import numpy as np
import ml_dtypes


def mxq(x, axis, fmt="e4m3"):
    dtype, down = {"e4m3": (ml_dtypes.float8_e4m3fn, 7), "e5m2": (ml_dtypes.float8_e5m2, 14)}[fmt]
    v = np.moveaxis(np.asarray(x, np.float32).astype(ml_dtypes.bfloat16).astype(np.float64), axis, -1)
    blocks = v.reshape(v.shape[:-1] + (-1, 32))
    amax = np.abs(blocks).max(-1, keepdims=True)
    byte = np.maximum(np.where(amax > 0, np.frexp(amax)[1] - 1 + 127, 0) - down, 1)
    scale = np.exp2(byte - 127.0)
    codes = (blocks / scale).astype(np.float32).astype(dtype).astype(np.float64)
    return np.moveaxis((codes * scale).reshape(v.shape), -1, axis)


WIDE = False


def mx_kscale(k):
    if not WIDE:
        return np.ones(k)
    levels = np.array([10, -10, 5, -5, 0])
    a = np.random.permutation(np.resize(levels, k // 512 * 4)).reshape(k // 512, 4)
    idx = np.arange(k)
    return np.exp2(a[idx // 512, idx % 128 // 32])


BF16 = ml_dtypes.bfloat16


def bf(x):
    return np.asarray(x, np.float32).astype(BF16)


def f64(x):
    return np.asarray(x).astype(np.float64)


B, S, DIM, QL, KVL, H, DN, DR, DV, P0 = 4, 2048, 512, 1536, 512, 4, 16, 128, 16, 37
EPS = 1e-6
HALF = DR // 2


def rms_norm(v, w):
    return v / np.sqrt(np.mean(v * v, axis=-1, keepdims=True) + EPS) * w


def rope(v, start):
    theta = 10000.0 ** (-np.arange(HALF) / HALF)
    pos = np.arange(v.shape[-2]) + start
    ang = pos[:, None] * theta[None, :]
    ang2 = np.concatenate([ang, ang], axis=-1)
    v1, v2 = v[..., :HALF], v[..., HALF:]
    rot = np.concatenate([-v2, v1], axis=-1)
    return v * np.cos(ang2) + rot * np.sin(ang2)


def setup_inputs():
    s = mx_kscale(DIM)
    return {"x": bf(np.random.standard_normal((B, S, DIM)) * s),
            "wkv_a": bf(np.random.standard_normal((DIM, KVL + DR)) / np.sqrt(DIM) / s[:, None]),
            "wkv_b": bf(np.random.standard_normal((KVL, H * (DN + DV))) / np.sqrt(KVL))}


def reference(x, wkv_a, wkv_b):
    kv = mxq(f64(x), 2, "e4m3") @ mxq(f64(wkv_a), 0, "e4m3")
    kv_c, k_pe = kv[..., :KVL], kv[..., KVL:]
    k_pe = rope(k_pe[:, :, None, :], P0)
    cn = rms_norm(kv_c, np.ones(KVL))
    kv_up = (mxq(cn, 2, "e4m3") @ mxq(f64(wkv_b), 0, "e4m3")).reshape(B, S, H, DN + DV)
    k_nope, v = kv_up[..., :DN], kv_up[..., DN:]
    k = np.concatenate([k_nope, np.broadcast_to(k_pe, (B, S, H, DR))], axis=-1)
    return k, v

@@ -1,0 +1,346 @@
+from contextlib import ExitStack
+
+import concourse.mybir as mybir
+from concourse.masks import make_identity
+
+F32 = mybir.dt.float32
+BF16 = mybir.dt.bfloat16
+U32 = mybir.dt.uint32
+U8 = mybir.dt.uint8
+FP8X4 = mybir.dt.float8_e4m3fn_x4
+ALU = mybir.AluOpType
+ACT = mybir.ActivationFunctionType
+
+P = 128
+PACK = 4
+TOKENS = 4 * 2048
+DIM = 512
+LATENT = 512
+ROPE = 128
+HALF = ROPE // 2
+HEADS = 4
+NOPE = 16
+VDIM = 16
+UP = HEADS * (NOPE + VDIM)
+KHEAD = NOPE + ROPE
+EPS = 1e-6
+POSITION = 37
+ROPE_BASE = 10000.0
+
+SUB = 4
+GROUP = SUB * P
+N_GROUPS = TOKENS // GROUP
+
+TWO_PI = 6.283185307179586
+
+FLOPS = 2 * TOKENS * DIM * (LATENT + ROPE) + 2 * TOKENS * LATENT * UP
+
+
+def cos_and_sin(angle):
+    y = angle - TWO_PI * round(angle / TWO_PI)
+    sums = [0.0, 0.0]
+    term = 1.0
+    for n in range(32):
+        sums[n % 2] += term if n % 4 < 2 else -term
+        term = term * y / (n + 1)
+    return sums[0], sums[1]
+
+
+def tile_mla_pb_t_kernel(tc, x, wkv_a, wkv_b, out_0, out_1):
+    nc = tc.nc
+    x_rows = x.rearrange("b s k -> (b s) k")
+    k_rows = out_0.rearrange("b s h d -> (b s) (h d)")
+    v_rows = out_1.rearrange("b s h d -> (b s) (h d)")
+
+    with ExitStack() as stack:
+        stack.enter_context(tc.manual_schedule())
+        consts = stack.enter_context(tc.tile_pool(name="consts", bufs=1))
+        x_pool = stack.enter_context(tc.tile_pool(name="x_pool", bufs=N_GROUPS))
+        grouped = stack.enter_context(tc.tile_pool(name="grouped", bufs=2))
+        x_mx = stack.enter_context(tc.tile_pool(name="x_mx", bufs=4))
+        cn_mx = stack.enter_context(tc.tile_pool(name="cn_mx", bufs=2))
+        scratch = stack.enter_context(tc.tile_pool(name="scratch", bufs=4))
+        stats = stack.enter_context(tc.tile_pool(name="stats", bufs=3))
+        work = stack.enter_context(tc.tile_pool(name="work", bufs=2))
+        outs = stack.enter_context(tc.tile_pool(name="outs", bufs=4))
+        tp_psum = stack.enter_context(tc.psum_pool(name="tp_psum", bufs=2))
+        ca_psum = stack.enter_context(tc.psum_pool(name="ca_psum", bufs=2))
+        cb_psum = stack.enter_context(tc.psum_pool(name="cb_psum", bufs=2))
+        sm_psum = stack.enter_context(tc.psum_pool(name="sm_psum", bufs=2))
+
+        wa_raw = consts.tile([P, PACK, LATENT + ROPE], BF16)
+        nc.sync.dma_start(
+            out=wa_raw[:].rearrange("p (u e) c -> p u (e c)", u=2),
+            in_=wkv_a.rearrange("(u p e) c -> p u (e c)", u=2, p=P, e=2),
+        )
+        x_sb = {}
+        for g in range(N_GROUPS):
+            x_sb[g] = x_pool.tile([P, SUB, DIM], BF16, name="x_sb")
+            nc.sync.dma_start(
+                out=x_sb[g][:],
+                in_=x_rows[g * GROUP : (g + 1) * GROUP, :].rearrange("(q i) k -> q i k", i=SUB),
+            )
+            if g == 0:
+                wb_raw = consts.tile([P, PACK, UP], BF16)
+                nc.sync.dma_start(out=wb_raw[:], in_=wkv_b.rearrange("(p t) n -> p t n", t=PACK))
+
+        ident = consts.tile([P, P], F32)
+        make_identity(nc, ident[:])
+        eps = consts.tile([P, 1], F32)
+        nc.vector.memset(eps[:], EPS)
+        ones = consts.tile([P, 2, HALF], F32)
+        nc.vector.memset(ones[:], 1.0)
+        table_warm = consts.tile([P, 1], F32)
+        nc.scalar.activation(out=table_warm[:], in_=eps[:], func=ACT.Sqrt)
+        cos_cos = consts.tile([P, 2, HALF], F32)
+        sin_pm = consts.tile([P, 2, HALF], F32)
+        for j in range(HALF):
+            cos_j, sin_j = cos_and_sin(POSITION * ROPE_BASE ** (-j / HALF))
+            nc.vector.tensor_scalar_mul(
+                out=cos_cos[:, :, j : j + 1], in0=ones[:, :, j : j + 1], scalar1=cos_j
+            )
+            nc.scalar.mul(out=sin_pm[:, 1, j : j + 1], in_=ones[:, 1, j : j + 1], mul=sin_j)
+        nc.scalar.mul(out=sin_pm[:, 0, :], in_=sin_pm[:, 1, :], mul=-1.0)
+        cos_all = cos_cos[:].rearrange("p a j -> p (a j)").unsqueeze(1).to_broadcast([P, SUB, ROPE])
+
+        wa_grp = consts.tile([P, LATENT + ROPE, PACK], BF16, align_bytes=64)
+        nc.vector.tensor_copy(
+            out=wa_grp[:, 0:LATENT, :].rearrange("p (t m) j -> p t m j", t=PACK),
+            in_=wa_raw[:, :, 0:LATENT].rearrange("p j (m t) -> p t m j", t=PACK),
+        )
+        nc.vector.tensor_copy(
+            out=wa_grp[:, LATENT:, :], in_=wa_raw[:, :, LATENT:].rearrange("p j c -> p c j")
+        )
+        wb_grp = consts.tile([P, UP, PACK], BF16, align_bytes=64)
+        nc.vector.tensor_copy(out=wb_grp[:], in_=wb_raw[:].rearrange("p j c -> p c j"))
+        wa_codes = consts.tile([P, LATENT + ROPE], U32, align_bytes=64)
+        wa_scales = consts.tile([P, LATENT + ROPE], U8, align_bytes=64)
+        wb_codes = consts.tile([P, UP], U32, align_bytes=64)
+        wb_scales = consts.tile([P, UP], U8, align_bytes=64)
+        nc.vector.quantize_mx(
+            out=wa_codes[:, 0:LATENT].bitcast(FP8X4),
+            scales=wa_scales[:, 0:LATENT],
+            in_=wa_grp[:, 0:LATENT, :].rearrange("p c j -> p (c j)"),
+        )
+        nc.vector.quantize_mx(
+            out=wa_codes[:, LATENT:].bitcast(FP8X4),
+            scales=wa_scales[:, LATENT:],
+            in_=wa_grp[:, LATENT:, :].rearrange("p c j -> p (c j)"),
+        )
+        nc.vector.quantize_mx(
+            out=wb_codes[:].bitcast(FP8X4),
+            scales=wb_scales[:],
+            in_=wb_grp[:].rearrange("p c j -> p (c j)"),
+        )
+
+        x_grp = {}
+        x_codes = {}
+        x_scales = {}
+        sumsq = {}
+        std = {}
+        rstd = {}
+        rstd_all = {}
+        r_ps = {}
+        cn_grp = {}
+        cn_codes = {}
+        cn_scales = {}
+        k_sb = {}
+        straight = {}
+        crossed = {}
+
+        def transpose_x(g):
+            x_grp[g] = grouped.tile([P, GROUP * PACK], BF16, name="x_grp", align_bytes=64)
+            words = x_grp[g][:].bitcast(F32).rearrange("p (i q u) -> p i q u", i=SUB, u=2)
+            for half in range(SUB // 2):
+                xt_ps = tp_psum.tile([P, 2, 2, P], F32, name="xt_ps", tag="tp")
+                for i2 in range(2):
+                    x_words = x_sb[g][:, 2 * half + i2, :].bitcast(F32)
+                    for u in range(2):
+                        nc.tensor.transpose(
+                            xt_ps[:, i2, u, :], x_words[:, u * P : (u + 1) * P], ident[:]
+                        )
+                nc.scalar.copy(
+                    out=words[:, 2 * half : 2 * half + 2, :, :],
+                    in_=xt_ps[:].rearrange("p i u q -> p i q u"),
+                )
+
+        def quantise_x(g):
+            x_codes[g] = x_mx.tile([P, GROUP], U32, name="x_codes", align_bytes=64)
+            x_scales[g] = x_mx.tile([P, GROUP], U8, name="x_scales", align_bytes=64)
+            nc.vector.quantize_mx(
+                out=x_codes[g][:].bitcast(FP8X4), scales=x_scales[g][:], in_=x_grp[g][:]
+            )
+
+        def first_product(g, i):
+            tok = slice(i * P, (i + 1) * P)
+            if i == 0:
+                sumsq[g] = stats.tile([P, SUB], F32, name="sumsq")
+            ca_ps = ca_psum.tile([P, LATENT], F32, name="ca_ps")
+            nc.tensor.matmul_mx(
+                out=ca_ps[:],
+                lhsT=x_codes[g][:, tok].bitcast(FP8X4),
+                lhsT_scale=x_scales[g][:, tok],
+                rhs=wa_codes[:, 0:LATENT].bitcast(FP8X4),
+                rhs_scale=wa_scales[:, 0:LATENT],
+                start=True,
+                stop=True,
+            )
+            squares = scratch.tile([P, LATENT], BF16, name="squares")
+            nc.scalar.activation(
+                out=squares[:], in_=ca_ps[:], func=ACT.Square, accum_out=sumsq[g][:, i : i + 1]
+            )
+
+        def rope_product(g):
+            r_ps[g] = sm_psum.tile([P, SUB, ROPE], F32, name="r_ps", tag="sm")
+            for i in range(SUB):
+                tok = slice(i * P, (i + 1) * P)
+                nc.tensor.matmul_mx(
+                    out=r_ps[g][:, i, :],
+                    lhsT=x_codes[g][:, tok].bitcast(FP8X4),
+                    lhsT_scale=x_scales[g][:, tok],
+                    rhs=wa_codes[:, LATENT:].bitcast(FP8X4),
+                    rhs_scale=wa_scales[:, LATENT:],
+                    start=True,
+                    stop=True,
+                )
+
+        def root_mean_square(g):
+            std[g] = stats.tile([P, SUB], F32, name="std")
+            nc.scalar.activation(
+                out=std[g][:], in_=sumsq[g][:], func=ACT.Sqrt, bias=eps[:], scale=1.0 / LATENT
+            )
+
+        def rotate_products(g):
+            straight[g] = work.tile([P, SUB, ROPE], F32, name="straight")
+            crossed[g] = work.tile([P, SUB, ROPE], F32, name="crossed")
+            nc.vector.tensor_tensor(out=straight[g][:], in0=r_ps[g][:], in1=cos_all, op=ALU.mult)
+            nc.vector.tensor_tensor(
+                out=crossed[g][:, :, 0:HALF],
+                in0=r_ps[g][:, :, HALF:ROPE],
+                in1=sin_pm[:, 0:1, :].to_broadcast([P, SUB, HALF]),
+                op=ALU.mult,
+            )
+            nc.vector.tensor_tensor(
+                out=crossed[g][:, :, HALF:ROPE],
+                in0=r_ps[g][:, :, 0:HALF],
+                in1=sin_pm[:, 1:2, :].to_broadcast([P, SUB, HALF]),
+                op=ALU.mult,
+            )
+
+        def rotate_sum(g):
+            k_sb[g] = outs.tile([P, SUB, HEADS, KHEAD], F32, name="k_sb")
+            nc.vector.tensor_tensor(
+                out=k_sb[g][:, :, 0, NOPE:KHEAD], in0=straight[g][:], in1=crossed[g][:], op=ALU.add
+            )
+
+        def repeat_for_heads(g):
+            nc.gpsimd.tensor_scalar(
+                out=k_sb[g][:, :, 1:HEADS, NOPE:KHEAD],
+                in0=k_sb[g][:, :, 0:1, NOPE:KHEAD].to_broadcast([P, SUB, HEADS - 1, ROPE]),
+                scalar1=1.0,
+                scalar2=0.0,
+                op0=ALU.mult,
+                op1=ALU.add,
+            )
+
+        def reciprocal_rms(g):
+            rstd[g] = stats.tile([P, SUB], F32, name="rstd")
+            nc.vector.reciprocal(out=rstd[g][:], in_=std[g][:])
+
+        def spread_rstd(g):
+            rstd_ps = tp_psum.tile([P, SUB, P], F32, name="rstd_ps", tag="tp")
+            for i in range(SUB):
+                nc.tensor.transpose(
+                    rstd_ps[:, i, :], rstd[g][:, i : i + 1].to_broadcast([P, P]), ident[:]
+                )
+            rstd_all[g] = work.tile([P, SUB, P], F32, name="rstd_all")
+            nc.scalar.copy(out=rstd_all[g][:], in_=rstd_ps[:])
+
+        def normalise(g, i):
+            tok = slice(i * P, (i + 1) * P)
+            if i == 0:
+                cn_grp[g] = grouped.tile([P, SUB, P, PACK], BF16, name="cn_grp", align_bytes=64)
+            cb_ps = cb_psum.tile([P, PACK, P], F32, name="cb_ps")
+            for t in range(PACK):
+                nc.tensor.matmul_mx(
+                    out=cb_ps[:, t, :],
+                    lhsT=wa_codes[:, t * P : (t + 1) * P].bitcast(FP8X4),
+                    lhsT_scale=wa_scales[:, t * P : (t + 1) * P],
+                    rhs=x_codes[g][:, tok].bitcast(FP8X4),
+                    rhs_scale=x_scales[g][:, tok],
+                    start=True,
+                    stop=True,
+                )
+            nc.vector.tensor_tensor(
+                out=cn_grp[g][:, i, :, :],
+                in0=cb_ps[:].rearrange("p t q -> p q t"),
+                in1=rstd_all[g][:, i, :].unsqueeze(2).to_broadcast([P, P, PACK]),
+                op=ALU.mult,
+            )
+
+        def quantise_cn(g):
+            cn_codes[g] = cn_mx.tile([P, GROUP], U32, name="cn_codes", align_bytes=64)
+            cn_scales[g] = cn_mx.tile([P, GROUP], U8, name="cn_scales", align_bytes=64)
+            nc.vector.quantize_mx(
+                out=cn_codes[g][:].bitcast(FP8X4),
+                scales=cn_scales[g][:],
+                in_=cn_grp[g][:].rearrange("p i q t -> p (i q t)"),
+            )
+
+        def second_product(g):
+            u_ps = sm_psum.tile([P, SUB, HEADS, NOPE + VDIM], F32, name="u_ps", tag="sm")
+            for i in range(SUB):
+                tok = slice(i * P, (i + 1) * P)
+                nc.tensor.matmul_mx(
+                    out=u_ps[:, i, :, :].rearrange("p h d -> p (h d)"),
+                    lhsT=cn_codes[g][:, tok].bitcast(FP8X4),
+                    lhsT_scale=cn_scales[g][:, tok],
+                    rhs=wb_codes[:].bitcast(FP8X4),
+                    rhs_scale=wb_scales[:],
+                    start=True,
+                    stop=True,
+                )
+            v_sb = outs.tile([P, SUB, HEADS, VDIM], F32, name="v_sb")
+            nc.scalar.copy(out=k_sb[g][:, :, :, 0:NOPE], in_=u_ps[:, :, :, 0:NOPE])
+            nc.scalar.copy(out=v_sb[:], in_=u_ps[:, :, :, NOPE:])
+            rows = slice(g * GROUP, (g + 1) * GROUP)
+            nc.sync.dma_start(
+                out=k_rows[rows, :].rearrange("(q i) c -> q (i c)", i=SUB),
+                in_=k_sb[g][:].rearrange("p i h d -> p (i h d)"),
+            )
+            nc.sync.dma_start(
+                out=v_rows[rows, :].rearrange("(q i) c -> q (i c)", i=SUB),
+                in_=v_sb[:].rearrange("p i h d -> p (i h d)"),
+            )
+
+        def live(g):
+            return 0 <= g < N_GROUPS
+
+        for step in range(-2, N_GROUPS + 3):
+            g_x, g_q, g_1, g_r, g_n, g_2 = step + 2, step + 1, step, step - 1, step - 2, step - 3
+            for i in range(SUB):
+                if i == SUB // 2:
+                    if live(g_2):
+                        second_product(g_2)
+                    if live(g_r):
+                        rotate_products(g_r)
+                if live(g_n):
+                    normalise(g_n, i)
+                if live(g_1):
+                    first_product(g_1, i)
+            if live(g_1):
+                rope_product(g_1)
+                root_mean_square(g_1)
+            if live(g_r):
+                rotate_sum(g_r)
+            if live(g_n):
+                quantise_cn(g_n)
+            if live(g_r):
+                repeat_for_heads(g_r)
+                spread_rstd(g_r)
+            if live(g_x):
+                transpose_x(g_x)
+            if live(g_q):
+                quantise_x(g_q)
+            if live(g_1):
+                reciprocal_rms(g_1)

@@ -53,7 +53,6 @@ def tile_mla_pb_t_kernel(tc, x, wkv_a, wkv_b, out_0, out_1):
     v_rows = out_1.rearrange("b s h d -> (b s) (h d)")
 
     with ExitStack() as stack:
-        stack.enter_context(tc.manual_schedule())
         consts = stack.enter_context(tc.tile_pool(name="consts", bufs=1))
         x_pool = stack.enter_context(tc.tile_pool(name="x_pool", bufs=N_GROUPS))
         grouped = stack.enter_context(tc.tile_pool(name="grouped", bufs=2))

@@ -234,8 +234,8 @@ def tile_mla_pb_t_kernel(tc, x, wkv_a, wkv_b, out_0, out_1):
 
         def repeat_for_heads(g):
             nc.gpsimd.tensor_scalar(
-                out=k_sb[g][:, :, 1:HEADS, NOPE:KHEAD],
-                in0=k_sb[g][:, :, 0:1, NOPE:KHEAD].to_broadcast([P, SUB, HEADS - 1, ROPE]),
+                out=k_sb[g][:, :, 2, NOPE:KHEAD],
+                in0=k_sb[g][:, :, 0, NOPE:KHEAD],
                 scalar1=1.0,
                 scalar2=0.0,
                 op0=ALU.mult,
@@ -303,9 +303,13 @@ def tile_mla_pb_t_kernel(tc, x, wkv_a, wkv_b, out_0, out_1):
             nc.scalar.copy(out=k_sb[g][:, :, :, 0:NOPE], in_=u_ps[:, :, :, 0:NOPE])
             nc.scalar.copy(out=v_sb[:], in_=u_ps[:, :, :, NOPE:])
             rows = slice(g * GROUP, (g + 1) * GROUP)
+            k_pairs = k_rows[rows, :].rearrange("(q i) (a c) -> q i a c", i=SUB, a=2)
+            sb_pairs = k_sb[g][:].rearrange("p i (a o) d -> p i a (o d)", o=2)
             nc.sync.dma_start(
-                out=k_rows[rows, :].rearrange("(q i) c -> q (i c)", i=SUB),
-                in_=k_sb[g][:].rearrange("p i h d -> p (i h d)"),
+                out=k_pairs[:, :, :, 0 : KHEAD + NOPE], in_=sb_pairs[:, :, :, 0 : KHEAD + NOPE]
+            )
+            nc.sync.dma_start(
+                out=k_pairs[:, :, :, KHEAD + NOPE :], in_=sb_pairs[:, :, :, NOPE:KHEAD]
             )
             nc.sync.dma_start(
                 out=v_rows[rows, :].rearrange("(q i) c -> q (i c)", i=SUB),

@@ -90,17 +90,21 @@ def tile_mla_pb_t_kernel(tc, x, wkv_a, wkv_b, out_0, out_1):
         ones = consts.tile([P, 2, HALF], F32)
         nc.vector.memset(ones[:], 1.0)
         table_warm = consts.tile([P, 1], F32)
-        nc.scalar.activation(out=table_warm[:], in_=eps[:], func=ACT.Sqrt)
-        cos_cos = consts.tile([P, 2, HALF], F32)
-        sin_pm = consts.tile([P, 2, HALF], F32)
+        nc.scalar.activation(out=table_warm[:], in_=eps[:], func=ACT.Abs_reciprocal_sqrt)
+        turns = consts.tile([P, 2, 2, HALF], F32)
         for j in range(HALF):
             cos_j, sin_j = cos_and_sin(POSITION * ROPE_BASE ** (-j / HALF))
             nc.vector.tensor_scalar_mul(
-                out=cos_cos[:, :, j : j + 1], in0=ones[:, :, j : j + 1], scalar1=cos_j
+                out=turns[:, 0, :, j : j + 1], in0=ones[:, :, j : j + 1], scalar1=cos_j
             )
-            nc.scalar.mul(out=sin_pm[:, 1, j : j + 1], in_=ones[:, 1, j : j + 1], mul=sin_j)
-        nc.scalar.mul(out=sin_pm[:, 0, :], in_=sin_pm[:, 1, :], mul=-1.0)
-        cos_all = cos_cos[:].rearrange("p a j -> p (a j)").unsqueeze(1).to_broadcast([P, SUB, ROPE])
+            nc.scalar.mul(out=turns[:, 1, 0, j : j + 1], in_=ones[:, 1, j : j + 1], mul=sin_j)
+        nc.scalar.mul(out=turns[:, 1, 1, :], in_=turns[:, 1, 0, :], mul=-1.0)
+        turns_all = (
+            turns[:]
+            .rearrange("p t a j -> p t (a j)")
+            .unsqueeze(1)
+            .to_broadcast([P, SUB, 2, ROPE])
+        )
 
         wa_grp = consts.tile([P, LATENT + ROPE, PACK], BF16, align_bytes=64)
         nc.vector.tensor_copy(
@@ -136,7 +140,6 @@ def tile_mla_pb_t_kernel(tc, x, wkv_a, wkv_b, out_0, out_1):
         x_codes = {}
         x_scales = {}
         sumsq = {}
-        std = {}
         rstd = {}
         rstd_all = {}
         r_ps = {}
@@ -144,8 +147,7 @@ def tile_mla_pb_t_kernel(tc, x, wkv_a, wkv_b, out_0, out_1):
         cn_codes = {}
         cn_scales = {}
         k_sb = {}
-        straight = {}
-        crossed = {}
+        turned = {}
 
         def transpose_x(g):
             x_grp[g] = grouped.tile([P, GROUP * PACK], BF16, name="x_grp", align_bytes=64)
@@ -203,33 +205,33 @@ def tile_mla_pb_t_kernel(tc, x, wkv_a, wkv_b, out_0, out_1):
                     stop=True,
                 )
 
-        def root_mean_square(g):
-            std[g] = stats.tile([P, SUB], F32, name="std")
+        def reciprocal_rms(g):
+            rstd[g] = stats.tile([P, SUB], F32, name="rstd")
             nc.scalar.activation(
-                out=std[g][:], in_=sumsq[g][:], func=ACT.Sqrt, bias=eps[:], scale=1.0 / LATENT
+                out=rstd[g][:],
+                in_=sumsq[g][:],
+                func=ACT.Abs_reciprocal_sqrt,
+                bias=eps[:],
+                scale=1.0 / LATENT,
             )
 
         def rotate_products(g):
-            straight[g] = work.tile([P, SUB, ROPE], F32, name="straight")
-            crossed[g] = work.tile([P, SUB, ROPE], F32, name="crossed")
-            nc.vector.tensor_tensor(out=straight[g][:], in0=r_ps[g][:], in1=cos_all, op=ALU.mult)
+            turned[g] = work.tile([P, SUB, 2, ROPE], F32, name="turned")
             nc.vector.tensor_tensor(
-                out=crossed[g][:, :, 0:HALF],
-                in0=r_ps[g][:, :, HALF:ROPE],
-                in1=sin_pm[:, 0:1, :].to_broadcast([P, SUB, HALF]),
-                op=ALU.mult,
-            )
-            nc.vector.tensor_tensor(
-                out=crossed[g][:, :, HALF:ROPE],
-                in0=r_ps[g][:, :, 0:HALF],
-                in1=sin_pm[:, 1:2, :].to_broadcast([P, SUB, HALF]),
+                out=turned[g][:],
+                in0=r_ps[g][:].unsqueeze(2).to_broadcast([P, SUB, 2, ROPE]),
+                in1=turns_all,
                 op=ALU.mult,
             )
 
         def rotate_sum(g):
             k_sb[g] = outs.tile([P, SUB, HEADS, KHEAD], F32, name="k_sb")
+            halves = turned[g][:].rearrange("p i t (a j) -> p i t a j", a=2)
             nc.vector.tensor_tensor(
-                out=k_sb[g][:, :, 0, NOPE:KHEAD], in0=straight[g][:], in1=crossed[g][:], op=ALU.add
+                out=k_sb[g][:, :, 0, NOPE:KHEAD].rearrange("p i (a j) -> p i a j", a=2),
+                in0=halves[:, :, 0, :, :],
+                in1=halves[:, :, 1, ::-1, :],
+                op=ALU.add,
             )
 
         def repeat_for_heads(g):
@@ -241,10 +243,6 @@ def tile_mla_pb_t_kernel(tc, x, wkv_a, wkv_b, out_0, out_1):
                 op0=ALU.mult,
                 op1=ALU.add,
             )
-
-        def reciprocal_rms(g):
-            rstd[g] = stats.tile([P, SUB], F32, name="rstd")
-            nc.vector.reciprocal(out=rstd[g][:], in_=std[g][:])
 
         def spread_rstd(g):
             rstd_ps = tp_psum.tile([P, SUB, P], F32, name="rstd_ps", tag="tp")
@@ -333,7 +331,7 @@ def tile_mla_pb_t_kernel(tc, x, wkv_a, wkv_b, out_0, out_1):
                     first_product(g_1, i)
             if live(g_1):
                 rope_product(g_1)
-                root_mean_square(g_1)
+                reciprocal_rms(g_1)
             if live(g_r):
                 rotate_sum(g_r)
             if live(g_n):
@@ -345,5 +343,3 @@ def tile_mla_pb_t_kernel(tc, x, wkv_a, wkv_b, out_0, out_1):
                 transpose_x(g_x)
             if live(g_q):
                 quantise_x(g_q)
-            if live(g_1):
-                reciprocal_rms(g_1)

@@ -30,6 +30,7 @@ ROPE_BASE = 10000.0
 SUB = 4
 GROUP = SUB * P
 N_GROUPS = TOKENS // GROUP
+LAST = N_GROUPS - 1
 
 TWO_PI = 6.283185307179586
 
@@ -51,6 +52,9 @@ def tile_mla_pb_t_kernel(tc, x, wkv_a, wkv_b, out_0, out_1):
     x_rows = x.rearrange("b s k -> (b s) k")
     k_rows = out_0.rearrange("b s h d -> (b s) (h d)")
     v_rows = out_1.rearrange("b s h d -> (b s) (h d)")
+
+    def rows_of(g):
+        return slice(g * GROUP, (g + 1) * GROUP)
 
     with ExitStack() as stack:
         consts = stack.enter_context(tc.tile_pool(name="consts", bufs=1))
@@ -235,9 +239,11 @@ def tile_mla_pb_t_kernel(tc, x, wkv_a, wkv_b, out_0, out_1):
             )
 
         def repeat_for_heads(g):
+            heads = slice(1, HEADS) if g == LAST else slice(2, 3)
+            n = heads.stop - heads.start
             nc.gpsimd.tensor_scalar(
-                out=k_sb[g][:, :, 2, NOPE:KHEAD],
-                in0=k_sb[g][:, :, 0, NOPE:KHEAD],
+                out=k_sb[g][:, :, heads, NOPE:KHEAD],
+                in0=k_sb[g][:, :, 0:1, NOPE:KHEAD].to_broadcast([P, SUB, n, ROPE]),
                 scalar1=1.0,
                 scalar2=0.0,
                 op0=ALU.mult,
@@ -275,21 +281,24 @@ def tile_mla_pb_t_kernel(tc, x, wkv_a, wkv_b, out_0, out_1):
                 op=ALU.mult,
             )
 
-        def quantise_cn(g):
-            cn_codes[g] = cn_mx.tile([P, GROUP], U32, name="cn_codes", align_bytes=64)
-            cn_scales[g] = cn_mx.tile([P, GROUP], U8, name="cn_scales", align_bytes=64)
+        def quantise_cn(g, low=0, high=SUB):
+            if low == 0:
+                cn_codes[g] = cn_mx.tile([P, GROUP], U32, name="cn_codes", align_bytes=64)
+                cn_scales[g] = cn_mx.tile([P, GROUP], U8, name="cn_scales", align_bytes=64)
+            tok = slice(low * P, high * P)
             nc.vector.quantize_mx(
-                out=cn_codes[g][:].bitcast(FP8X4),
-                scales=cn_scales[g][:],
-                in_=cn_grp[g][:].rearrange("p i q t -> p (i q t)"),
+                out=cn_codes[g][:, tok].bitcast(FP8X4),
+                scales=cn_scales[g][:, tok],
+                in_=cn_grp[g][:, low:high, :, :].rearrange("p i q t -> p (i q t)"),
             )
 
-        def second_product(g):
-            u_ps = sm_psum.tile([P, SUB, HEADS, NOPE + VDIM], F32, name="u_ps", tag="sm")
-            for i in range(SUB):
+        def second_product(g, low=0, high=SUB):
+            n = high - low
+            u_ps = sm_psum.tile([P, n, HEADS, NOPE + VDIM], F32, name="u_ps", tag="sm")
+            for i in range(low, high):
                 tok = slice(i * P, (i + 1) * P)
                 nc.tensor.matmul_mx(
-                    out=u_ps[:, i, :, :].rearrange("p h d -> p (h d)"),
+                    out=u_ps[:, i - low, :, :].rearrange("p h d -> p (h d)"),
                     lhsT=cn_codes[g][:, tok].bitcast(FP8X4),
                     lhsT_scale=cn_scales[g][:, tok],
                     rhs=wb_codes[:].bitcast(FP8X4),
@@ -297,48 +306,63 @@ def tile_mla_pb_t_kernel(tc, x, wkv_a, wkv_b, out_0, out_1):
                     start=True,
                     stop=True,
                 )
-            v_sb = outs.tile([P, SUB, HEADS, VDIM], F32, name="v_sb")
-            nc.scalar.copy(out=k_sb[g][:, :, :, 0:NOPE], in_=u_ps[:, :, :, 0:NOPE])
+            v_sb = outs.tile([P, n, HEADS, VDIM], F32, name="v_sb")
+            nc.scalar.copy(out=k_sb[g][:, low:high, :, 0:NOPE], in_=u_ps[:, :, :, 0:NOPE])
             nc.scalar.copy(out=v_sb[:], in_=u_ps[:, :, :, NOPE:])
-            rows = slice(g * GROUP, (g + 1) * GROUP)
-            k_pairs = k_rows[rows, :].rearrange("(q i) (a c) -> q i a c", i=SUB, a=2)
-            sb_pairs = k_sb[g][:].rearrange("p i (a o) d -> p i a (o d)", o=2)
+            if g == LAST:
+                k_quads = k_rows[rows_of(g), :].rearrange("(q i) c -> q i c", i=SUB)
+                nc.sync.dma_start(
+                    out=k_quads[:, low:high, :],
+                    in_=k_sb[g][:, low:high, :, :].rearrange("p i h d -> p i (h d)"),
+                )
+            else:
+                k_pairs = k_rows[rows_of(g), :].rearrange("(q i) (a c) -> q i a c", i=SUB, a=2)
+                sb_pairs = k_sb[g][:].rearrange("p i (a o) d -> p i a (o d)", o=2)
+                nc.sync.dma_start(
+                    out=k_pairs[:, :, :, 0 : KHEAD + NOPE],
+                    in_=sb_pairs[:, :, :, 0 : KHEAD + NOPE],
+                )
+                nc.sync.dma_start(
+                    out=k_pairs[:, :, :, KHEAD + NOPE :], in_=sb_pairs[:, :, :, NOPE:KHEAD]
+                )
+            v_quads = v_rows[rows_of(g), :].rearrange("(q i) c -> q i c", i=SUB)
             nc.sync.dma_start(
-                out=k_pairs[:, :, :, 0 : KHEAD + NOPE], in_=sb_pairs[:, :, :, 0 : KHEAD + NOPE]
-            )
-            nc.sync.dma_start(
-                out=k_pairs[:, :, :, KHEAD + NOPE :], in_=sb_pairs[:, :, :, NOPE:KHEAD]
-            )
-            nc.sync.dma_start(
-                out=v_rows[rows, :].rearrange("(q i) c -> q (i c)", i=SUB),
-                in_=v_sb[:].rearrange("p i h d -> p (i h d)"),
+                out=v_quads[:, low:high, :], in_=v_sb[:].rearrange("p i h d -> p i (h d)")
             )
 
         def live(g):
             return 0 <= g < N_GROUPS
 
-        for step in range(-2, N_GROUPS + 3):
+        for step in range(-2, N_GROUPS + 2):
             g_x, g_q, g_1, g_r, g_n, g_2 = step + 2, step + 1, step, step - 1, step - 2, step - 3
+            if live(g_1):
+                rope_product(g_1)
+            if live(g_r):
+                spread_rstd(g_r)
             for i in range(SUB):
                 if i == SUB // 2:
-                    if live(g_2):
+                    if live(g_2) and g_2 < LAST:
                         second_product(g_2)
                     if live(g_r):
                         rotate_products(g_r)
                 if live(g_n):
                     normalise(g_n, i)
+                if g_n == LAST and i == 2:
+                    quantise_cn(LAST, 0, 2)
                 if live(g_1):
                     first_product(g_1, i)
             if live(g_1):
-                rope_product(g_1)
                 reciprocal_rms(g_1)
             if live(g_r):
                 rotate_sum(g_r)
-            if live(g_n):
+            if g_n == LAST:
+                second_product(LAST, 0, 2)
+                quantise_cn(LAST, 2, 4)
+                second_product(LAST, 2, 4)
+            elif live(g_n):
                 quantise_cn(g_n)
             if live(g_r):
                 repeat_for_heads(g_r)
-                spread_rstd(g_r)
             if live(g_x):
                 transpose_x(g_x)
             if live(g_q):

from contextlib import ExitStack

import concourse.mybir as mybir
from concourse.masks import make_identity

F32 = mybir.dt.float32
BF16 = mybir.dt.bfloat16
U32 = mybir.dt.uint32
U8 = mybir.dt.uint8
FP8X4 = mybir.dt.float8_e4m3fn_x4
ALU = mybir.AluOpType
ACT = mybir.ActivationFunctionType

P = 128
PACK = 4
TOKENS = 4 * 2048
DIM = 512
LATENT = 512
ROPE = 128
HALF = ROPE // 2
HEADS = 4
NOPE = 16
VDIM = 16
UP = HEADS * (NOPE + VDIM)
KHEAD = NOPE + ROPE
EPS = 1e-6
POSITION = 37
ROPE_BASE = 10000.0

SUB = 4
GROUP = SUB * P
N_GROUPS = TOKENS // GROUP
LAST = N_GROUPS - 1

TWO_PI = 6.283185307179586

FLOPS = 2 * TOKENS * DIM * (LATENT + ROPE) + 2 * TOKENS * LATENT * UP


def cos_and_sin(angle):
    y = angle - TWO_PI * round(angle / TWO_PI)
    sums = [0.0, 0.0]
    term = 1.0
    for n in range(32):
        sums[n % 2] += term if n % 4 < 2 else -term
        term = term * y / (n + 1)
    return sums[0], sums[1]


def tile_mla_pb_t_kernel(tc, x, wkv_a, wkv_b, out_0, out_1):
    nc = tc.nc
    x_rows = x.rearrange("b s k -> (b s) k")
    k_rows = out_0.rearrange("b s h d -> (b s) (h d)")
    v_rows = out_1.rearrange("b s h d -> (b s) (h d)")

    def rows_of(g):
        return slice(g * GROUP, (g + 1) * GROUP)

    with ExitStack() as stack:
        consts = stack.enter_context(tc.tile_pool(name="consts", bufs=1))
        x_pool = stack.enter_context(tc.tile_pool(name="x_pool", bufs=N_GROUPS))
        grouped = stack.enter_context(tc.tile_pool(name="grouped", bufs=2))
        x_mx = stack.enter_context(tc.tile_pool(name="x_mx", bufs=4))
        cn_mx = stack.enter_context(tc.tile_pool(name="cn_mx", bufs=2))
        scratch = stack.enter_context(tc.tile_pool(name="scratch", bufs=4))
        stats = stack.enter_context(tc.tile_pool(name="stats", bufs=3))
        work = stack.enter_context(tc.tile_pool(name="work", bufs=2))
        outs = stack.enter_context(tc.tile_pool(name="outs", bufs=4))
        tp_psum = stack.enter_context(tc.psum_pool(name="tp_psum", bufs=2))
        ca_psum = stack.enter_context(tc.psum_pool(name="ca_psum", bufs=2))
        cb_psum = stack.enter_context(tc.psum_pool(name="cb_psum", bufs=2))
        sm_psum = stack.enter_context(tc.psum_pool(name="sm_psum", bufs=2))

        wa_raw = consts.tile([P, PACK, LATENT + ROPE], BF16)
        nc.sync.dma_start(
            out=wa_raw[:].rearrange("p (u e) c -> p u (e c)", u=2),
            in_=wkv_a.rearrange("(u p e) c -> p u (e c)", u=2, p=P, e=2),
        )
        x_sb = {}
        for g in range(N_GROUPS):
            x_sb[g] = x_pool.tile([P, SUB, DIM], BF16, name="x_sb")
            nc.sync.dma_start(
                out=x_sb[g][:],
                in_=x_rows[g * GROUP : (g + 1) * GROUP, :].rearrange("(q i) k -> q i k", i=SUB),
            )
            if g == 0:
                wb_raw = consts.tile([P, PACK, UP], BF16)
                nc.sync.dma_start(out=wb_raw[:], in_=wkv_b.rearrange("(p t) n -> p t n", t=PACK))

        ident = consts.tile([P, P], F32)
        make_identity(nc, ident[:])
        eps = consts.tile([P, 1], F32)
        nc.vector.memset(eps[:], EPS)
        ones = consts.tile([P, 2, HALF], F32)
        nc.vector.memset(ones[:], 1.0)
        table_warm = consts.tile([P, 1], F32)
        nc.scalar.activation(out=table_warm[:], in_=eps[:], func=ACT.Abs_reciprocal_sqrt)
        turns = consts.tile([P, 2, 2, HALF], F32)
        for j in range(HALF):
            cos_j, sin_j = cos_and_sin(POSITION * ROPE_BASE ** (-j / HALF))
            nc.vector.tensor_scalar_mul(
                out=turns[:, 0, :, j : j + 1], in0=ones[:, :, j : j + 1], scalar1=cos_j
            )
            nc.scalar.mul(out=turns[:, 1, 0, j : j + 1], in_=ones[:, 1, j : j + 1], mul=sin_j)
        nc.scalar.mul(out=turns[:, 1, 1, :], in_=turns[:, 1, 0, :], mul=-1.0)
        turns_all = (
            turns[:]
            .rearrange("p t a j -> p t (a j)")
            .unsqueeze(1)
            .to_broadcast([P, SUB, 2, ROPE])
        )

        wa_grp = consts.tile([P, LATENT + ROPE, PACK], BF16, align_bytes=64)
        nc.vector.tensor_copy(
            out=wa_grp[:, 0:LATENT, :].rearrange("p (t m) j -> p t m j", t=PACK),
            in_=wa_raw[:, :, 0:LATENT].rearrange("p j (m t) -> p t m j", t=PACK),
        )
        nc.vector.tensor_copy(
            out=wa_grp[:, LATENT:, :], in_=wa_raw[:, :, LATENT:].rearrange("p j c -> p c j")
        )
        wb_grp = consts.tile([P, UP, PACK], BF16, align_bytes=64)
        nc.vector.tensor_copy(out=wb_grp[:], in_=wb_raw[:].rearrange("p j c -> p c j"))
        wa_codes = consts.tile([P, LATENT + ROPE], U32, align_bytes=64)
        wa_scales = consts.tile([P, LATENT + ROPE], U8, align_bytes=64)
        wb_codes = consts.tile([P, UP], U32, align_bytes=64)
        wb_scales = consts.tile([P, UP], U8, align_bytes=64)
        nc.vector.quantize_mx(
            out=wa_codes[:, 0:LATENT].bitcast(FP8X4),
            scales=wa_scales[:, 0:LATENT],
            in_=wa_grp[:, 0:LATENT, :].rearrange("p c j -> p (c j)"),
        )
        nc.vector.quantize_mx(
            out=wa_codes[:, LATENT:].bitcast(FP8X4),
            scales=wa_scales[:, LATENT:],
            in_=wa_grp[:, LATENT:, :].rearrange("p c j -> p (c j)"),
        )
        nc.vector.quantize_mx(
            out=wb_codes[:].bitcast(FP8X4),
            scales=wb_scales[:],
            in_=wb_grp[:].rearrange("p c j -> p (c j)"),
        )

        x_grp = {}
        x_codes = {}
        x_scales = {}
        sumsq = {}
        rstd = {}
        rstd_all = {}
        r_ps = {}
        cn_grp = {}
        cn_codes = {}
        cn_scales = {}
        k_sb = {}
        turned = {}

        def transpose_x(g):
            x_grp[g] = grouped.tile([P, GROUP * PACK], BF16, name="x_grp", align_bytes=64)
            words = x_grp[g][:].bitcast(F32).rearrange("p (i q u) -> p i q u", i=SUB, u=2)
            for half in range(SUB // 2):
                xt_ps = tp_psum.tile([P, 2, 2, P], F32, name="xt_ps", tag="tp")
                for i2 in range(2):
                    x_words = x_sb[g][:, 2 * half + i2, :].bitcast(F32)
                    for u in range(2):
                        nc.tensor.transpose(
                            xt_ps[:, i2, u, :], x_words[:, u * P : (u + 1) * P], ident[:]
                        )
                nc.scalar.copy(
                    out=words[:, 2 * half : 2 * half + 2, :, :],
                    in_=xt_ps[:].rearrange("p i u q -> p i q u"),
                )

        def quantise_x(g):
            x_codes[g] = x_mx.tile([P, GROUP], U32, name="x_codes", align_bytes=64)
            x_scales[g] = x_mx.tile([P, GROUP], U8, name="x_scales", align_bytes=64)
            nc.vector.quantize_mx(
                out=x_codes[g][:].bitcast(FP8X4), scales=x_scales[g][:], in_=x_grp[g][:]
            )

        def first_product(g, i):
            tok = slice(i * P, (i + 1) * P)
            if i == 0:
                sumsq[g] = stats.tile([P, SUB], F32, name="sumsq")
            ca_ps = ca_psum.tile([P, LATENT], F32, name="ca_ps")
            nc.tensor.matmul_mx(
                out=ca_ps[:],
                lhsT=x_codes[g][:, tok].bitcast(FP8X4),
                lhsT_scale=x_scales[g][:, tok],
                rhs=wa_codes[:, 0:LATENT].bitcast(FP8X4),
                rhs_scale=wa_scales[:, 0:LATENT],
                start=True,
                stop=True,
            )
            squares = scratch.tile([P, LATENT], BF16, name="squares")
            nc.scalar.activation(
                out=squares[:], in_=ca_ps[:], func=ACT.Square, accum_out=sumsq[g][:, i : i + 1]
            )

        def rope_product(g):
            r_ps[g] = sm_psum.tile([P, SUB, ROPE], F32, name="r_ps", tag="sm")
            for i in range(SUB):
                tok = slice(i * P, (i + 1) * P)
                nc.tensor.matmul_mx(
                    out=r_ps[g][:, i, :],
                    lhsT=x_codes[g][:, tok].bitcast(FP8X4),
                    lhsT_scale=x_scales[g][:, tok],
                    rhs=wa_codes[:, LATENT:].bitcast(FP8X4),
                    rhs_scale=wa_scales[:, LATENT:],
                    start=True,
                    stop=True,
                )

        def reciprocal_rms(g):
            rstd[g] = stats.tile([P, SUB], F32, name="rstd")
            nc.scalar.activation(
                out=rstd[g][:],
                in_=sumsq[g][:],
                func=ACT.Abs_reciprocal_sqrt,
                bias=eps[:],
                scale=1.0 / LATENT,
            )

        def rotate_products(g):
            turned[g] = work.tile([P, SUB, 2, ROPE], F32, name="turned")
            nc.vector.tensor_tensor(
                out=turned[g][:],
                in0=r_ps[g][:].unsqueeze(2).to_broadcast([P, SUB, 2, ROPE]),
                in1=turns_all,
                op=ALU.mult,
            )

        def rotate_sum(g):
            k_sb[g] = outs.tile([P, SUB, HEADS, KHEAD], F32, name="k_sb")
            halves = turned[g][:].rearrange("p i t (a j) -> p i t a j", a=2)
            nc.vector.tensor_tensor(
                out=k_sb[g][:, :, 0, NOPE:KHEAD].rearrange("p i (a j) -> p i a j", a=2),
                in0=halves[:, :, 0, :, :],
                in1=halves[:, :, 1, ::-1, :],
                op=ALU.add,
            )

        def repeat_for_heads(g):
            heads = slice(1, HEADS) if g == LAST else slice(2, 3)
            n = heads.stop - heads.start
            nc.gpsimd.tensor_scalar(
                out=k_sb[g][:, :, heads, NOPE:KHEAD],
                in0=k_sb[g][:, :, 0:1, NOPE:KHEAD].to_broadcast([P, SUB, n, ROPE]),
                scalar1=1.0,
                scalar2=0.0,
                op0=ALU.mult,
                op1=ALU.add,
            )

        def spread_rstd(g):
            rstd_ps = tp_psum.tile([P, SUB, P], F32, name="rstd_ps", tag="tp")
            for i in range(SUB):
                nc.tensor.transpose(
                    rstd_ps[:, i, :], rstd[g][:, i : i + 1].to_broadcast([P, P]), ident[:]
                )
            rstd_all[g] = work.tile([P, SUB, P], F32, name="rstd_all")
            nc.scalar.copy(out=rstd_all[g][:], in_=rstd_ps[:])

        def normalise(g, i):
            tok = slice(i * P, (i + 1) * P)
            if i == 0:
                cn_grp[g] = grouped.tile([P, SUB, P, PACK], BF16, name="cn_grp", align_bytes=64)
            cb_ps = cb_psum.tile([P, PACK, P], F32, name="cb_ps")
            for t in range(PACK):
                nc.tensor.matmul_mx(
                    out=cb_ps[:, t, :],
                    lhsT=wa_codes[:, t * P : (t + 1) * P].bitcast(FP8X4),
                    lhsT_scale=wa_scales[:, t * P : (t + 1) * P],
                    rhs=x_codes[g][:, tok].bitcast(FP8X4),
                    rhs_scale=x_scales[g][:, tok],
                    start=True,
                    stop=True,
                )
            nc.vector.tensor_tensor(
                out=cn_grp[g][:, i, :, :],
                in0=cb_ps[:].rearrange("p t q -> p q t"),
                in1=rstd_all[g][:, i, :].unsqueeze(2).to_broadcast([P, P, PACK]),
                op=ALU.mult,
            )

        def quantise_cn(g, low=0, high=SUB):
            if low == 0:
                cn_codes[g] = cn_mx.tile([P, GROUP], U32, name="cn_codes", align_bytes=64)
                cn_scales[g] = cn_mx.tile([P, GROUP], U8, name="cn_scales", align_bytes=64)
            tok = slice(low * P, high * P)
            nc.vector.quantize_mx(
                out=cn_codes[g][:, tok].bitcast(FP8X4),
                scales=cn_scales[g][:, tok],
                in_=cn_grp[g][:, low:high, :, :].rearrange("p i q t -> p (i q t)"),
            )

        def second_product(g, low=0, high=SUB):
            n = high - low
            u_ps = sm_psum.tile([P, n, HEADS, NOPE + VDIM], F32, name="u_ps", tag="sm")
            for i in range(low, high):
                tok = slice(i * P, (i + 1) * P)
                nc.tensor.matmul_mx(
                    out=u_ps[:, i - low, :, :].rearrange("p h d -> p (h d)"),
                    lhsT=cn_codes[g][:, tok].bitcast(FP8X4),
                    lhsT_scale=cn_scales[g][:, tok],
                    rhs=wb_codes[:].bitcast(FP8X4),
                    rhs_scale=wb_scales[:],
                    start=True,
                    stop=True,
                )
            v_sb = outs.tile([P, n, HEADS, VDIM], F32, name="v_sb")
            nc.scalar.copy(out=k_sb[g][:, low:high, :, 0:NOPE], in_=u_ps[:, :, :, 0:NOPE])
            nc.scalar.copy(out=v_sb[:], in_=u_ps[:, :, :, NOPE:])
            if g == LAST:
                k_quads = k_rows[rows_of(g), :].rearrange("(q i) c -> q i c", i=SUB)
                nc.sync.dma_start(
                    out=k_quads[:, low:high, :],
                    in_=k_sb[g][:, low:high, :, :].rearrange("p i h d -> p i (h d)"),
                )
            else:
                k_pairs = k_rows[rows_of(g), :].rearrange("(q i) (a c) -> q i a c", i=SUB, a=2)
                sb_pairs = k_sb[g][:].rearrange("p i (a o) d -> p i a (o d)", o=2)
                nc.sync.dma_start(
                    out=k_pairs[:, :, :, 0 : KHEAD + NOPE],
                    in_=sb_pairs[:, :, :, 0 : KHEAD + NOPE],
                )
                nc.sync.dma_start(
                    out=k_pairs[:, :, :, KHEAD + NOPE :], in_=sb_pairs[:, :, :, NOPE:KHEAD]
                )
            v_quads = v_rows[rows_of(g), :].rearrange("(q i) c -> q i c", i=SUB)
            nc.sync.dma_start(
                out=v_quads[:, low:high, :], in_=v_sb[:].rearrange("p i h d -> p i (h d)")
            )

        def live(g):
            return 0 <= g < N_GROUPS

        for step in range(-2, N_GROUPS + 2):
            g_x, g_q, g_1, g_r, g_n, g_2 = step + 2, step + 1, step, step - 1, step - 2, step - 3
            if live(g_1):
                rope_product(g_1)
            if live(g_r):
                spread_rstd(g_r)
            for i in range(SUB):
                if i == SUB // 2:
                    if live(g_2) and g_2 < LAST:
                        second_product(g_2)
                    if live(g_r):
                        rotate_products(g_r)
                if live(g_n):
                    normalise(g_n, i)
                if g_n == LAST and i == 2:
                    quantise_cn(LAST, 0, 2)
                if live(g_1):
                    first_product(g_1, i)
            if live(g_1):
                reciprocal_rms(g_1)
            if live(g_r):
                rotate_sum(g_r)
            if g_n == LAST:
                second_product(LAST, 0, 2)
                quantise_cn(LAST, 2, 4)
                second_product(LAST, 2, 4)
            elif live(g_n):
                quantise_cn(g_n)
            if live(g_r):
                repeat_for_heads(g_r)
            if live(g_x):
                transpose_x(g_x)
            if live(g_q):
                quantise_x(g_q)
